import numpy as np
import ml_dtypes

BF16 = ml_dtypes.bfloat16


def bf(x):
    return np.asarray(x, np.float32).astype(BF16)


def f32(x):
    return np.asarray(x, np.float32)


def f64(x):
    return np.asarray(x).astype(np.float64)


def striped(idx):
    return np.tile(idx.reshape(-1, 16).T, (8, 1))


C, S, N, T, E = 512, 2048, 1024, 128, 1536
BASE = 10000.0


def sinusoid():
    dim = np.arange(C // 2, dtype=np.float32)
    p = np.arange(1, T + 1, dtype=np.float32)
    ang = p[None, :] / np.power(np.float32(BASE), np.float32(2.0) * dim / np.float32(C))[:, None]
    tab = np.zeros((C, T), np.float32)
    tab[0::2] = np.sin(ang)
    tab[1::2] = np.cos(ang)
    return tab


def setup_inputs():
    return {"emb": f32(np.random.standard_normal((C, S))), "pos": f32(sinusoid()), "wqkv": bf(0.02 * np.random.standard_normal((C, E))), "bqkv": f32(0.1 * np.random.standard_normal((E, 1))), "offs": striped(np.random.permutation(np.tile(np.arange(S), 2))[:N])}


def reference(emb, pos, wqkv, bqkv, offs):
    idx = offs[:16].T.reshape(-1)
    x = f64(emb)[:, idx] + np.tile(f64(pos), (1, N // T))
    return np.concatenate([x, f64(wqkv).T @ x + f64(bqkv)], axis=0)

@@ -1,0 +1,87 @@
+import concourse.mybir as mybir
+
+F32, BF16, U16 = mybir.dt.float32, mybir.dt.bfloat16, mybir.dt.uint16
+ADD = mybir.AluOpType.add
+COPY = mybir.ActivationFunctionType.Copy
+IDENTITY = mybir.ActivationFunctionType.Identity
+
+P = 128
+C, S, N, T, E = 512, 2048, 1024, 128, 1536
+KB = C // P
+MB = E // P
+QB = 4
+HALF = 512
+NH = N // HALF
+
+FLOPS = 2 * C * E * N
+
+
+def tile_plaindecoder_kernel(tc, emb, pos, wqkv, bqkv, offs, out):
+    nc = tc.nc
+    with (
+        tc.tile_pool(name="held", bufs=1) as held,
+        tc.tile_pool(name="stage", bufs=6) as stage,
+        tc.psum_pool(name="psum", bufs=8) as psum,
+    ):
+        offsets = held.tile([P, N // 16], U16, name="offsets")
+        nc.sync.dma_start(offsets[:], offs)
+        pos_sb = held.tile([P, KB, T], F32, name="pos_sb")
+        nc.sync.dma_start(pos_sb[:], pos.rearrange("(k p) t -> p k t", p=P))
+        emb_sb = [held.tile([P, S], F32, name=f"emb{k}") for k in range(KB)]
+        w_q = held.tile([P, KB, QB * P], BF16, name="w_q")
+        w_kv = held.tile([P, KB, (MB - QB) * P], BF16, name="w_kv")
+        bias = held.tile([P, MB], F32, name="bias")
+        nc.sync.dma_start(emb_sb[0][:], emb[0:P, :])
+        nc.sync.dma_start(w_q[:], wqkv[:, 0 : QB * P].rearrange("(k p) e -> p k e", p=P))
+        for k in range(1, KB):
+            nc.sync.dma_start(emb_sb[k][:], emb[k * P : (k + 1) * P, :])
+        nc.sync.dma_start(w_kv[:], wqkv[:, QB * P : E].rearrange("(k p) e -> p k e", p=P))
+        with nc.allow_non_contiguous_dma(reason="bias: one float32 to a partition, 12 columns"):
+            nc.sync.dma_start(bias[:], bqkv.rearrange("(m p) o -> p (m o)", p=P))
+
+        pos_rep = [held.tile([P, HALF // T, T], F32, name=f"pos_rep{k}") for k in range(KB)]
+        for k in range(KB):
+            nc.scalar.activation(
+                pos_rep[k][:], pos_sb[:, k, :].unsqueeze(1).to_broadcast([P, HALF // T, T]), COPY
+            )
+
+        x32 = [held.tile([P, N], F32, name=f"x32_{k}") for k in range(KB)]
+        x16 = [held.tile([P, N], BF16, name=f"x16_{k}") for k in range(KB)]
+        q_acc = [[psum.tile([P, HALF], F32, name="acc") for h in range(NH)] for m in range(QB)]
+        for k in range(KB):
+            for h in range(NH):
+                cols = slice(h * HALF, (h + 1) * HALF)
+                piece = offsets[:, h * (HALF // 16) : (h + 1) * (HALF // 16)]
+                nc.vector.tensor_tensor(x32[k][:, cols], emb_sb[k][:].indirect(piece), pos_rep[k][:], ADD)
+                nc.scalar.activation(x16[k][:, cols], x32[k][:, cols], COPY)
+                for m in range(QB):
+                    nc.tensor.matmul(
+                        q_acc[m][h][:],
+                        w_q[:, k, m * P : (m + 1) * P],
+                        x16[k][:, cols],
+                        start=(k == 0),
+                        stop=(k == KB - 1),
+                    )
+            nc.sync.dma_start(out[k * P : (k + 1) * P, :], x32[k][:])
+
+        for m in range(MB):
+            for h in range(NH):
+                cols = slice(h * HALF, (h + 1) * HALF)
+                if m < QB:
+                    acc = q_acc[m][h]
+                else:
+                    acc = psum.tile([P, HALF], F32, name="acc")
+                    for k in range(KB):
+                        nc.tensor.matmul(
+                            acc[:],
+                            w_kv[:, k, (m - QB) * P : (m - QB + 1) * P],
+                            x16[k][:, cols],
+                            start=(k == 0),
+                            stop=(k == KB - 1),
+                        )
+                y = stage.tile([P, HALF], F32, name="y")
+                if h == 0:
+                    nc.scalar.activation(y[:], acc[:], IDENTITY, bias=bias[:, m : m + 1])
+                else:
+                    nc.vector.tensor_scalar_add(y[:], acc[:], bias[:, m : m + 1])
+                nc.sync.dma_start(out[C + m * P : C + (m + 1) * P, cols], y[:])

@@ -12,6 +12,7 @@ MB = E // P
 QB = 4
 HALF = 512
 NH = N // HALF
+WARM = 24
 
 FLOPS = 2 * C * E * N
 
@@ -38,6 +39,12 @@ def tile_plaindecoder_kernel(tc, emb, pos, wqkv, bqkv, offs, out):
         nc.sync.dma_start(w_kv[:], wqkv[:, QB * P : E].rearrange("(k p) e -> p k e", p=P))
         with nc.allow_non_contiguous_dma(reason="bias: one float32 to a partition, 12 columns"):
             nc.sync.dma_start(bias[:], bqkv.rearrange("(m p) o -> p (m o)", p=P))
+
+        zeros = held.tile([P, HALF], BF16, name="zeros")
+        nc.vector.memset(zeros[:], 0.0)
+        unread = psum.tile([P, HALF], F32, name="acc")
+        for i in range(WARM):
+            nc.tensor.matmul(unread[:], zeros[:, 0:P], zeros[:], start=True, stop=True)
 
         pos_rep = [held.tile([P, HALF // T, T], F32, name=f"pos_rep{k}") for k in range(KB)]
         for k in range(KB):

@@ -12,7 +12,6 @@ MB = E // P
 QB = 4
 HALF = 512
 NH = N // HALF
-WARM = 24
 
 FLOPS = 2 * C * E * N
 
@@ -26,25 +25,28 @@ def tile_plaindecoder_kernel(tc, emb, pos, wqkv, bqkv, offs, out):
     ):
         offsets = held.tile([P, N // 16], U16, name="offsets")
         nc.sync.dma_start(offsets[:], offs)
+        bias_row = held.tile([1, E], F32, name="bias_row")
+        nc.sync.dma_start(bias_row[:], bqkv.rearrange("e o -> o e"))
         pos_sb = held.tile([P, KB, T], F32, name="pos_sb")
         nc.sync.dma_start(pos_sb[:], pos.rearrange("(k p) t -> p k t", p=P))
         emb_sb = [held.tile([P, S], F32, name=f"emb{k}") for k in range(KB)]
         w_q = held.tile([P, KB, QB * P], BF16, name="w_q")
         w_kv = held.tile([P, KB, (MB - QB) * P], BF16, name="w_kv")
-        bias = held.tile([P, MB], F32, name="bias")
         nc.sync.dma_start(emb_sb[0][:], emb[0:P, :])
         nc.sync.dma_start(w_q[:], wqkv[:, 0 : QB * P].rearrange("(k p) e -> p k e", p=P))
         for k in range(1, KB):
             nc.sync.dma_start(emb_sb[k][:], emb[k * P : (k + 1) * P, :])
         nc.sync.dma_start(w_kv[:], wqkv[:, QB * P : E].rearrange("(k p) e -> p k e", p=P))
-        with nc.allow_non_contiguous_dma(reason="bias: one float32 to a partition, 12 columns"):
-            nc.sync.dma_start(bias[:], bqkv.rearrange("(m p) o -> p (m o)", p=P))
 
-        zeros = held.tile([P, HALF], BF16, name="zeros")
-        nc.vector.memset(zeros[:], 0.0)
-        unread = psum.tile([P, HALF], F32, name="acc")
-        for i in range(WARM):
-            nc.tensor.matmul(unread[:], zeros[:, 0:P], zeros[:], start=True, stop=True)
+        one = held.tile([1, 1], F32, name="one")
+        nc.vector.memset(one[:], 1.0)
+        bias_ps = psum.tile([P, MB], F32, name="bias_ps", tag="acc")
+        for m in range(MB):
+            nc.tensor.matmul(
+                bias_ps[:, m : m + 1], bias_row[:, m * P : (m + 1) * P], one[:], start=True, stop=True
+            )
+        bias = held.tile([P, MB], F32, name="bias")
+        nc.vector.tensor_copy(bias[:], bias_ps[:])
 
         pos_rep = [held.tile([P, HALF // T, T], F32, name=f"pos_rep{k}") for k in range(KB)]
         for k in range(KB):

@@ -23,10 +23,12 @@ def tile_plaindecoder_kernel(tc, emb, pos, wqkv, bqkv, offs, out):
         tc.tile_pool(name="stage", bufs=6) as stage,
         tc.psum_pool(name="psum", bufs=8) as psum,
     ):
+        bias = held.tile([P, MB], F32, name="bias")
+        with nc.allow_non_contiguous_dma(reason="one float32 to a partition"):
+            nc.scalar.dma_start(bias[:], bqkv.rearrange("(m p) o -> p (m o)", p=P))
+
         offsets = held.tile([P, N // 16], U16, name="offsets")
         nc.sync.dma_start(offsets[:], offs)
-        bias_row = held.tile([1, E], F32, name="bias_row")
-        nc.sync.dma_start(bias_row[:], bqkv.rearrange("e o -> o e"))
         pos_sb = held.tile([P, KB, T], F32, name="pos_sb")
         nc.sync.dma_start(pos_sb[:], pos.rearrange("(k p) t -> p k t", p=P))
         emb_sb = [held.tile([P, S], F32, name=f"emb{k}") for k in range(KB)]
@@ -37,16 +39,6 @@ def tile_plaindecoder_kernel(tc, emb, pos, wqkv, bqkv, offs, out):
         for k in range(1, KB):
             nc.sync.dma_start(emb_sb[k][:], emb[k * P : (k + 1) * P, :])
         nc.sync.dma_start(w_kv[:], wqkv[:, QB * P : E].rearrange("(k p) e -> p k e", p=P))
-
-        one = held.tile([1, 1], F32, name="one")
-        nc.vector.memset(one[:], 1.0)
-        bias_ps = psum.tile([P, MB], F32, name="bias_ps", tag="acc")
-        for m in range(MB):
-            nc.tensor.matmul(
-                bias_ps[:, m : m + 1], bias_row[:, m * P : (m + 1) * P], one[:], start=True, stop=True
-            )
-        bias = held.tile([P, MB], F32, name="bias")
-        nc.vector.tensor_copy(bias[:], bias_ps[:])
 
         pos_rep = [held.tile([P, HALF // T, T], F32, name=f"pos_rep{k}") for k in range(KB)]
         for k in range(KB):

@@ -18,27 +18,28 @@ FLOPS = 2 * C * E * N
 
 def tile_plaindecoder_kernel(tc, emb, pos, wqkv, bqkv, offs, out):
     nc = tc.nc
+    emb_v = emb.rearrange("(p k) s -> p k s", k=KB)
+    pos_v = pos.rearrange("(p k) t -> p k t", k=KB)
+    w_v = wqkv.rearrange("(p k) e -> p k e", k=KB)
+    x_v = out[0:C, :].rearrange("(p k) n -> p k n", k=KB)
     with (
         tc.tile_pool(name="held", bufs=1) as held,
-        tc.tile_pool(name="stage", bufs=6) as stage,
         tc.psum_pool(name="psum", bufs=8) as psum,
     ):
-        bias = held.tile([P, MB], F32, name="bias")
-        with nc.allow_non_contiguous_dma(reason="one float32 to a partition"):
-            nc.scalar.dma_start(bias[:], bqkv.rearrange("(m p) o -> p (m o)", p=P))
-
         offsets = held.tile([P, N // 16], U16, name="offsets")
         nc.sync.dma_start(offsets[:], offs)
         pos_sb = held.tile([P, KB, T], F32, name="pos_sb")
-        nc.sync.dma_start(pos_sb[:], pos.rearrange("(k p) t -> p k t", p=P))
+        nc.sync.dma_start(pos_sb[:], pos_v)
         emb_sb = [held.tile([P, S], F32, name=f"emb{k}") for k in range(KB)]
-        w_q = held.tile([P, KB, QB * P], BF16, name="w_q")
+        w_q = [held.tile([P, QB * P], BF16, name=f"w_q{k}") for k in range(KB)]
+        for k in range(KB):
+            nc.sync.dma_start(emb_sb[k][:], emb_v[:, k, :])
+            nc.sync.dma_start(w_q[k][:], w_v[:, k, 0 : QB * P])
         w_kv = held.tile([P, KB, (MB - QB) * P], BF16, name="w_kv")
-        nc.sync.dma_start(emb_sb[0][:], emb[0:P, :])
-        nc.sync.dma_start(w_q[:], wqkv[:, 0 : QB * P].rearrange("(k p) e -> p k e", p=P))
-        for k in range(1, KB):
-            nc.sync.dma_start(emb_sb[k][:], emb[k * P : (k + 1) * P, :])
-        nc.sync.dma_start(w_kv[:], wqkv[:, QB * P : E].rearrange("(k p) e -> p k e", p=P))
+        nc.sync.dma_start(w_kv[:], w_v[:, :, QB * P : E])
+        bias = held.tile([P, MB], F32, name="bias")
+        with nc.allow_non_contiguous_dma(reason="bias: one float32 to a partition, 12 columns"):
+            nc.sync.dma_start(bias[:], bqkv.rearrange("(m p) o -> p (m o)", p=P))
 
         pos_rep = [held.tile([P, HALF // T, T], F32, name=f"pos_rep{k}") for k in range(KB)]
         for k in range(KB):
@@ -46,43 +47,46 @@ def tile_plaindecoder_kernel(tc, emb, pos, wqkv, bqkv, offs, out):
                 pos_rep[k][:], pos_sb[:, k, :].unsqueeze(1).to_broadcast([P, HALF // T, T]), COPY
             )
 
-        x32 = [held.tile([P, N], F32, name=f"x32_{k}") for k in range(KB)]
+        def add_bias_and_store(acc, m, first, width, engine):
+            y = held.tile([P, width], F32, name=f"y{m}_{first}")
+            if engine == 0:
+                nc.scalar.activation(y[:], acc[:], IDENTITY, bias=bias[:, m : m + 1])
+            else:
+                nc.vector.tensor_scalar_add(y[:], acc[:], bias[:, m : m + 1])
+            nc.sync.dma_start(out[C + m * P : C + (m + 1) * P, first : first + width], y[:])
+
+        x32 = held.tile([P, KB, N], F32, name="x32")
         x16 = [held.tile([P, N], BF16, name=f"x16_{k}") for k in range(KB)]
         q_acc = [[psum.tile([P, HALF], F32, name="acc") for h in range(NH)] for m in range(QB)]
         for k in range(KB):
             for h in range(NH):
                 cols = slice(h * HALF, (h + 1) * HALF)
                 piece = offsets[:, h * (HALF // 16) : (h + 1) * (HALF // 16)]
-                nc.vector.tensor_tensor(x32[k][:, cols], emb_sb[k][:].indirect(piece), pos_rep[k][:], ADD)
-                nc.scalar.activation(x16[k][:, cols], x32[k][:, cols], COPY)
+                nc.vector.tensor_tensor(x32[:, k, cols], emb_sb[k][:].indirect(piece), pos_rep[k][:], ADD)
+                nc.scalar.activation(x16[k][:, cols], x32[:, k, cols], COPY)
                 for m in range(QB):
                     nc.tensor.matmul(
                         q_acc[m][h][:],
-                        w_q[:, k, m * P : (m + 1) * P],
+                        w_q[k][:, m * P : (m + 1) * P],
                         x16[k][:, cols],
                         start=(k == 0),
                         stop=(k == KB - 1),
                     )
-            nc.sync.dma_start(out[k * P : (k + 1) * P, :], x32[k][:])
-
-        for m in range(MB):
+        nc.sync.dma_start(x_v, x32[:])
+        for m in range(QB):
             for h in range(NH):
-                cols = slice(h * HALF, (h + 1) * HALF)
-                if m < QB:
-                    acc = q_acc[m][h]
-                else:
-                    acc = psum.tile([P, HALF], F32, name="acc")
-                    for k in range(KB):
-                        nc.tensor.matmul(
-                            acc[:],
-                            w_kv[:, k, (m - QB) * P : (m - QB + 1) * P],
-                            x16[k][:, cols],
-                            start=(k == 0),
-                            stop=(k == KB - 1),
-                        )
-                y = stage.tile([P, HALF], F32, name="y")
-                if h == 0:
-                    nc.scalar.activation(y[:], acc[:], IDENTITY, bias=bias[:, m : m + 1])
-                else:
-                    nc.vector.tensor_scalar_add(y[:], acc[:], bias[:, m : m + 1])
-                nc.sync.dma_start(out[C + m * P : C + (m + 1) * P, cols], y[:])
+                add_bias_and_store(q_acc[m][h], m, h * HALF, HALF, h)
+
+        for m in range(QB, MB):
+            width = HALF if m < MB - 1 else HALF // 2
+            for j in range(N // width):
+                acc = psum.tile([P, width], F32, name="acc")
+                for k in range(KB):
+                    nc.tensor.matmul(
+                        acc[:],
+                        w_kv[:, k, (m - QB) * P : (m - QB + 1) * P],
+                        x16[k][:, j * width : (j + 1) * width],
+                        start=(k == 0),
+                        stop=(k == KB - 1),
+                    )
+                add_bias_and_store(acc, m, j * width, width, j % 2)

@@ -1,4 +1,5 @@
 import concourse.mybir as mybir
+from concourse.masks import make_identity
 
 F32, BF16, U16 = mybir.dt.float32, mybir.dt.bfloat16, mybir.dt.uint16
 ADD = mybir.AluOpType.add
@@ -28,6 +29,8 @@ def tile_plaindecoder_kernel(tc, emb, pos, wqkv, bqkv, offs, out):
     ):
         offsets = held.tile([P, N // 16], U16, name="offsets")
         nc.sync.dma_start(offsets[:], offs)
+        bias_rows = held.tile([MB, P], F32, name="bias_rows")
+        nc.sync.dma_start(bias_rows[:], bqkv.rearrange("(m p) o -> m (p o)", p=P))
         pos_sb = held.tile([P, KB, T], F32, name="pos_sb")
         nc.sync.dma_start(pos_sb[:], pos_v)
         emb_sb = [held.tile([P, S], F32, name=f"emb{k}") for k in range(KB)]
@@ -37,23 +40,19 @@ def tile_plaindecoder_kernel(tc, emb, pos, wqkv, bqkv, offs, out):
             nc.sync.dma_start(w_q[k][:], w_v[:, k, 0 : QB * P])
         w_kv = held.tile([P, KB, (MB - QB) * P], BF16, name="w_kv")
         nc.sync.dma_start(w_kv[:], w_v[:, :, QB * P : E])
+
+        eye = held.tile([MB, MB], F32, name="eye")
+        make_identity(nc, eye[:])
+        bias_ps = psum.tile([P, MB], F32, name="bias_ps", tag="acc")
+        nc.tensor.matmul(bias_ps[:], bias_rows[:], eye[:], start=True, stop=True)
         bias = held.tile([P, MB], F32, name="bias")
-        with nc.allow_non_contiguous_dma(reason="bias: one float32 to a partition, 12 columns"):
-            nc.sync.dma_start(bias[:], bqkv.rearrange("(m p) o -> p (m o)", p=P))
+        nc.vector.tensor_copy(bias[:], bias_ps[:])
 
         pos_rep = [held.tile([P, HALF // T, T], F32, name=f"pos_rep{k}") for k in range(KB)]
         for k in range(KB):
             nc.scalar.activation(
                 pos_rep[k][:], pos_sb[:, k, :].unsqueeze(1).to_broadcast([P, HALF // T, T]), COPY
             )
-
-        def add_bias_and_store(acc, m, first, width, engine):
-            y = held.tile([P, width], F32, name=f"y{m}_{first}")
-            if engine == 0:
-                nc.scalar.activation(y[:], acc[:], IDENTITY, bias=bias[:, m : m + 1])
-            else:
-                nc.vector.tensor_scalar_add(y[:], acc[:], bias[:, m : m + 1])
-            nc.sync.dma_start(out[C + m * P : C + (m + 1) * P, first : first + width], y[:])
 
         x32 = held.tile([P, KB, N], F32, name="x32")
         x16 = [held.tile([P, N], BF16, name=f"x16_{k}") for k in range(KB)]
@@ -73,20 +72,30 @@ def tile_plaindecoder_kernel(tc, emb, pos, wqkv, bqkv, offs, out):
                         stop=(k == KB - 1),
                     )
         nc.sync.dma_start(x_v, x32[:])
-        for m in range(QB):
-            for h in range(NH):
-                add_bias_and_store(q_acc[m][h], m, h * HALF, HALF, h)
 
-        for m in range(QB, MB):
+        for m in range(MB):
             width = HALF if m < MB - 1 else HALF // 2
+            y = held.tile([P, N], F32, name=f"y{m}")
+            y_rows = out[C + m * P : C + (m + 1) * P, :]
             for j in range(N // width):
-                acc = psum.tile([P, width], F32, name="acc")
-                for k in range(KB):
-                    nc.tensor.matmul(
-                        acc[:],
-                        w_kv[:, k, (m - QB) * P : (m - QB + 1) * P],
-                        x16[k][:, j * width : (j + 1) * width],
-                        start=(k == 0),
-                        stop=(k == KB - 1),
-                    )
-                add_bias_and_store(acc, m, j * width, width, j % 2)
+                cols = slice(j * width, (j + 1) * width)
+                if m < QB:
+                    acc = q_acc[m][j]
+                else:
+                    acc = psum.tile([P, width], F32, name="acc")
+                    for k in range(KB):
+                        nc.tensor.matmul(
+                            acc[:],
+                            w_kv[:, k, (m - QB) * P : (m - QB + 1) * P],
+                            x16[k][:, cols],
+                            start=(k == 0),
+                            stop=(k == KB - 1),
+                        )
+                if j % 2 == 0:
+                    nc.scalar.activation(y[:, cols], acc[:], IDENTITY, bias=bias[:, m : m + 1])
+                else:
+                    nc.vector.tensor_scalar_add(y[:, cols], acc[:], bias[:, m : m + 1])
+                if m == MB - 1:
+                    nc.sync.dma_start(y_rows[:, cols], y[:, cols])
+            if m < MB - 1:
+                nc.sync.dma_start(y_rows, y[:])

@@ -1,5 +1,4 @@
 import concourse.mybir as mybir
-from concourse.masks import make_identity
 
 F32, BF16, U16 = mybir.dt.float32, mybir.dt.bfloat16, mybir.dt.uint16
 ADD = mybir.AluOpType.add
@@ -29,8 +28,6 @@ def tile_plaindecoder_kernel(tc, emb, pos, wqkv, bqkv, offs, out):
     ):
         offsets = held.tile([P, N // 16], U16, name="offsets")
         nc.sync.dma_start(offsets[:], offs)
-        bias_rows = held.tile([MB, P], F32, name="bias_rows")
-        nc.sync.dma_start(bias_rows[:], bqkv.rearrange("(m p) o -> m (p o)", p=P))
         pos_sb = held.tile([P, KB, T], F32, name="pos_sb")
         nc.sync.dma_start(pos_sb[:], pos_v)
         emb_sb = [held.tile([P, S], F32, name=f"emb{k}") for k in range(KB)]
@@ -38,21 +35,26 @@ def tile_plaindecoder_kernel(tc, emb, pos, wqkv, bqkv, offs, out):
         for k in range(KB):
             nc.sync.dma_start(emb_sb[k][:], emb_v[:, k, :])
             nc.sync.dma_start(w_q[k][:], w_v[:, k, 0 : QB * P])
-        w_kv = held.tile([P, KB, (MB - QB) * P], BF16, name="w_kv")
-        nc.sync.dma_start(w_kv[:], w_v[:, :, QB * P : E])
-
-        eye = held.tile([MB, MB], F32, name="eye")
-        make_identity(nc, eye[:])
-        bias_ps = psum.tile([P, MB], F32, name="bias_ps", tag="acc")
-        nc.tensor.matmul(bias_ps[:], bias_rows[:], eye[:], start=True, stop=True)
         bias = held.tile([P, MB], F32, name="bias")
-        nc.vector.tensor_copy(bias[:], bias_ps[:])
+        with nc.allow_non_contiguous_dma(reason="bias: one float32 to a partition, 12 columns"):
+            nc.sync.dma_start(bias[:], bqkv.rearrange("(m p) o -> p (m o)", p=P))
+        w_kv = [held.tile([P, KB, QB * P], BF16, name=f"w_kv{g}") for g in range(2)]
+        for g in range(2):
+            nc.sync.dma_start(w_kv[g][:], w_v[:, :, (g + 1) * QB * P : (g + 2) * QB * P])
 
         pos_rep = [held.tile([P, HALF // T, T], F32, name=f"pos_rep{k}") for k in range(KB)]
         for k in range(KB):
             nc.scalar.activation(
                 pos_rep[k][:], pos_sb[:, k, :].unsqueeze(1).to_broadcast([P, HALF // T, T]), COPY
             )
+
+        def add_bias_and_store(acc, m, first, width, engine):
+            y = held.tile([P, width], F32, name=f"y{m}_{first}")
+            if engine == 0:
+                nc.scalar.activation(y[:], acc[:], IDENTITY, bias=bias[:, m : m + 1])
+            else:
+                nc.vector.tensor_scalar_add(y[:], acc[:], bias[:, m : m + 1])
+            nc.sync.dma_start(out[C + m * P : C + (m + 1) * P, first : first + width], y[:])
 
         x32 = held.tile([P, KB, N], F32, name="x32")
         x16 = [held.tile([P, N], BF16, name=f"x16_{k}") for k in range(KB)]
@@ -72,30 +74,20 @@ def tile_plaindecoder_kernel(tc, emb, pos, wqkv, bqkv, offs, out):
                         stop=(k == KB - 1),
                     )
         nc.sync.dma_start(x_v, x32[:])
+        for m in range(QB):
+            for h in range(NH):
+                add_bias_and_store(q_acc[m][h], m, h * HALF, HALF, h)
 
-        for m in range(MB):
+        for m in range(QB, MB):
             width = HALF if m < MB - 1 else HALF // 2
-            y = held.tile([P, N], F32, name=f"y{m}")
-            y_rows = out[C + m * P : C + (m + 1) * P, :]
             for j in range(N // width):
-                cols = slice(j * width, (j + 1) * width)
-                if m < QB:
-                    acc = q_acc[m][j]
-                else:
-                    acc = psum.tile([P, width], F32, name="acc")
-                    for k in range(KB):
-                        nc.tensor.matmul(
-                            acc[:],
-                            w_kv[:, k, (m - QB) * P : (m - QB + 1) * P],
-                            x16[k][:, cols],
-                            start=(k == 0),
-                            stop=(k == KB - 1),
-                        )
-                if j % 2 == 0:
-                    nc.scalar.activation(y[:, cols], acc[:], IDENTITY, bias=bias[:, m : m + 1])
-                else:
-                    nc.vector.tensor_scalar_add(y[:, cols], acc[:], bias[:, m : m + 1])
-                if m == MB - 1:
-                    nc.sync.dma_start(y_rows[:, cols], y[:, cols])
-            if m < MB - 1:
-                nc.sync.dma_start(y_rows, y[:])
+                acc = psum.tile([P, width], F32, name="acc")
+                for k in range(KB):
+                    nc.tensor.matmul(
+                        acc[:],
+                        w_kv[m // QB - 1][:, k, (m % QB) * P : (m % QB + 1) * P],
+                        x16[k][:, j * width : (j + 1) * width],
+                        start=(k == 0),
+                        stop=(k == KB - 1),
+                    )
+                add_bias_and_store(acc, m, j * width, width, j % 2)

@@ -12,6 +12,7 @@ MB = E // P
 QB = 4
 HALF = 512
 NH = N // HALF
+QUARTER = HALF // 2
 
 FLOPS = 2 * C * E * N
 
@@ -60,18 +61,22 @@ def tile_plaindecoder_kernel(tc, emb, pos, wqkv, bqkv, offs, out):
         x16 = [held.tile([P, N], BF16, name=f"x16_{k}") for k in range(KB)]
         q_acc = [[psum.tile([P, HALF], F32, name="acc") for h in range(NH)] for m in range(QB)]
         for k in range(KB):
-            for h in range(NH):
-                cols = slice(h * HALF, (h + 1) * HALF)
-                piece = offsets[:, h * (HALF // 16) : (h + 1) * (HALF // 16)]
-                nc.vector.tensor_tensor(x32[:, k, cols], emb_sb[k][:].indirect(piece), pos_rep[k][:], ADD)
+            width = QUARTER if k in (0, KB - 1) else HALF
+            for first in range(0, N, width):
+                cols = slice(first, first + width)
+                piece = offsets[:, first // 16 : (first + width) // 16]
+                nc.vector.tensor_tensor(
+                    x32[:, k, cols], emb_sb[k][:].indirect(piece), pos_rep[k][:, 0 : width // T, :], ADD
+                )
                 nc.scalar.activation(x16[k][:, cols], x32[:, k, cols], COPY)
+                h, inside = divmod(first, HALF)
                 for m in range(QB):
                     nc.tensor.matmul(
-                        q_acc[m][h][:],
+                        q_acc[m][h][:, inside : inside + width],
                         w_q[k][:, m * P : (m + 1) * P],
                         x16[k][:, cols],
-                        start=(k == 0),
-                        stop=(k == KB - 1),
+                        start=(k == 0 and inside == 0),
+                        stop=(k == KB - 1 and inside + width == HALF),
                     )
         nc.sync.dma_start(x_v, x32[:])
         for m in range(QB):

@@ -61,7 +61,7 @@ def tile_plaindecoder_kernel(tc, emb, pos, wqkv, bqkv, offs, out):
         x16 = [held.tile([P, N], BF16, name=f"x16_{k}") for k in range(KB)]
         q_acc = [[psum.tile([P, HALF], F32, name="acc") for h in range(NH)] for m in range(QB)]
         for k in range(KB):
-            width = QUARTER if k in (0, KB - 1) else HALF
+            width = QUARTER
             for first in range(0, N, width):
                 cols = slice(first, first + width)
                 piece = offsets[:, first // 16 : (first + width) // 16]

@@ -30,12 +30,14 @@ def tile_plaindecoder_kernel(tc, emb, pos, wqkv, bqkv, offs, out):
         offsets = held.tile([P, N // 16], U16, name="offsets")
         nc.sync.dma_start(offsets[:], offs)
         pos_sb = held.tile([P, KB, T], F32, name="pos_sb")
-        nc.sync.dma_start(pos_sb[:], pos_v)
+        nc.sync.dma_start(pos_sb[:, 0 : KB // 2, :], pos_v[:, 0 : KB // 2, :])
         emb_sb = [held.tile([P, S], F32, name=f"emb{k}") for k in range(KB)]
         w_q = [held.tile([P, QB * P], BF16, name=f"w_q{k}") for k in range(KB)]
         for k in range(KB):
             nc.sync.dma_start(emb_sb[k][:], emb_v[:, k, :])
             nc.sync.dma_start(w_q[k][:], w_v[:, k, 0 : QB * P])
+            if k == 0:
+                nc.sync.dma_start(pos_sb[:, KB // 2 : KB, :], pos_v[:, KB // 2 : KB, :])
         bias = held.tile([P, MB], F32, name="bias")
         with nc.allow_non_contiguous_dma(reason="bias: one float32 to a partition, 12 columns"):
             nc.sync.dma_start(bias[:], bqkv.rearrange("(m p) o -> p (m o)", p=P))
@@ -84,15 +86,17 @@ def tile_plaindecoder_kernel(tc, emb, pos, wqkv, bqkv, offs, out):
                 add_bias_and_store(q_acc[m][h], m, h * HALF, HALF, h)
 
         for m in range(QB, MB):
-            width = HALF if m < MB - 1 else HALF // 2
-            for j in range(N // width):
+            widths = [HALF, HALF] if m < MB - 1 else [HALF, HALF - T, T]
+            first = 0
+            for j, width in enumerate(widths):
                 acc = psum.tile([P, width], F32, name="acc")
                 for k in range(KB):
                     nc.tensor.matmul(
                         acc[:],
                         w_kv[m // QB - 1][:, k, (m % QB) * P : (m % QB + 1) * P],
-                        x16[k][:, j * width : (j + 1) * width],
+                        x16[k][:, first : first + width],
                         start=(k == 0),
                         stop=(k == KB - 1),
                     )
-                add_bias_and_store(acc, m, j * width, width, j % 2)
+                add_bias_and_store(acc, m, first, width, (len(widths) - j) % 2)
+                first += width

@@ -63,8 +63,9 @@ def tile_plaindecoder_kernel(tc, emb, pos, wqkv, bqkv, offs, out):
         x16 = [held.tile([P, N], BF16, name=f"x16_{k}") for k in range(KB)]
         q_acc = [[psum.tile([P, HALF], F32, name="acc") for h in range(NH)] for m in range(QB)]
         for k in range(KB):
-            width = QUARTER
-            for first in range(0, N, width):
+            widths = [QUARTER] * 4 if k < KB - 1 else [QUARTER] * 3 + [T, T]
+            for i, width in enumerate(widths):
+                first = sum(widths[:i])
                 cols = slice(first, first + width)
                 piece = offsets[:, first // 16 : (first + width) // 16]
                 nc.vector.tensor_tensor(

@@ -84,7 +84,7 @@ def tile_plaindecoder_kernel(tc, emb, pos, wqkv, bqkv, offs, out):
         nc.sync.dma_start(x_v, x32[:])
         for m in range(QB):
             for h in range(NH):
-                add_bias_and_store(q_acc[m][h], m, h * HALF, HALF, h)
+                add_bias_and_store(q_acc[m][h], m, h * HALF, HALF, 1 - h)
 
         for m in range(QB, MB):
             widths = [HALF, HALF] if m < MB - 1 else [HALF, HALF - T, T]

@@ -63,7 +63,11 @@ def tile_plaindecoder_kernel(tc, emb, pos, wqkv, bqkv, offs, out):
         x16 = [held.tile([P, N], BF16, name=f"x16_{k}") for k in range(KB)]
         q_acc = [[psum.tile([P, HALF], F32, name="acc") for h in range(NH)] for m in range(QB)]
         for k in range(KB):
-            widths = [QUARTER] * 4 if k < KB - 1 else [QUARTER] * 3 + [T, T]
+            widths = [QUARTER] * 4
+            if k == 0:
+                widths = [T, T] + [QUARTER] * 3
+            if k == KB - 1:
+                widths = [QUARTER] * 3 + [T, T]
             for i, width in enumerate(widths):
                 first = sum(widths[:i])
                 cols = slice(first, first + width)

@@ -1,4 +1,5 @@
 import concourse.mybir as mybir
+from concourse.masks import make_identity
 
 F32, BF16, U16 = mybir.dt.float32, mybir.dt.bfloat16, mybir.dt.uint16
 ADD = mybir.AluOpType.add
@@ -13,6 +14,8 @@ QB = 4
 HALF = 512
 NH = N // HALF
 QUARTER = HALF // 2
+BR = 4
+BJ = MB // BR
 
 FLOPS = 2 * C * E * N
 
@@ -29,6 +32,8 @@ def tile_plaindecoder_kernel(tc, emb, pos, wqkv, bqkv, offs, out):
     ):
         offsets = held.tile([P, N // 16], U16, name="offsets")
         nc.sync.dma_start(offsets[:], offs)
+        bias_rows = held.tile([BR, BJ * P], F32, name="bias_rows")
+        nc.scalar.dma_start(bias_rows[:], bqkv.rearrange("(r f) o -> r (f o)", r=BR))
         pos_sb = held.tile([P, KB, T], F32, name="pos_sb")
         nc.sync.dma_start(pos_sb[:, 0 : KB // 2, :], pos_v[:, 0 : KB // 2, :])
         emb_sb = [held.tile([P, S], F32, name=f"emb{k}") for k in range(KB)]
@@ -38,12 +43,17 @@ def tile_plaindecoder_kernel(tc, emb, pos, wqkv, bqkv, offs, out):
             nc.sync.dma_start(w_q[k][:], w_v[:, k, 0 : QB * P])
             if k == 0:
                 nc.sync.dma_start(pos_sb[:, KB // 2 : KB, :], pos_v[:, KB // 2 : KB, :])
-        bias = held.tile([P, MB], F32, name="bias")
-        with nc.allow_non_contiguous_dma(reason="bias: one float32 to a partition, 12 columns"):
-            nc.sync.dma_start(bias[:], bqkv.rearrange("(m p) o -> p (m o)", p=P))
         w_kv = [held.tile([P, KB, QB * P], BF16, name=f"w_kv{g}") for g in range(2)]
         for g in range(2):
             nc.sync.dma_start(w_kv[g][:], w_v[:, :, (g + 1) * QB * P : (g + 2) * QB * P])
+
+        identity = held.tile([BR, BR], F32, name="identity")
+        make_identity(nc, identity[:])
+        bias_t = psum.tile([P, BJ, BR], F32, name="bias_t", tag="acc")
+        for j in range(BJ):
+            nc.tensor.matmul(bias_t[:, j, :], bias_rows[:, j * P : (j + 1) * P], identity[:])
+        bias = held.tile([P, BJ, BR], F32, name="bias")
+        nc.vector.tensor_copy(bias[:], bias_t[:])
 
         pos_rep = [held.tile([P, HALF // T, T], F32, name=f"pos_rep{k}") for k in range(KB)]
         for k in range(KB):
@@ -53,10 +63,12 @@ def tile_plaindecoder_kernel(tc, emb, pos, wqkv, bqkv, offs, out):
 
         def add_bias_and_store(acc, m, first, width, engine):
             y = held.tile([P, width], F32, name=f"y{m}_{first}")
+            r, j = divmod(m, BJ)
+            bias_m = bias[:, j, r : r + 1]
             if engine == 0:
-                nc.scalar.activation(y[:], acc[:], IDENTITY, bias=bias[:, m : m + 1])
+                nc.scalar.activation(y[:], acc[:], IDENTITY, bias=bias_m)
             else:
-                nc.vector.tensor_scalar_add(y[:], acc[:], bias[:, m : m + 1])
+                nc.vector.tensor_scalar_add(y[:], acc[:], bias_m)
             nc.sync.dma_start(out[C + m * P : C + (m + 1) * P, first : first + width], y[:])
 
         x32 = held.tile([P, KB, N], F32, name="x32")

@@ -14,6 +14,7 @@ QB = 4
 HALF = 512
 NH = N // HALF
 QUARTER = HALF // 2
+LAST = 224
 BR = 4
 BJ = MB // BR
 
@@ -61,15 +62,20 @@ def tile_plaindecoder_kernel(tc, emb, pos, wqkv, bqkv, offs, out):
                 pos_rep[k][:], pos_sb[:, k, :].unsqueeze(1).to_broadcast([P, HALF // T, T]), COPY
             )
 
+        y = [held.tile([P, N], F32, name=f"y{m}") for m in range(MB)]
+
         def add_bias_and_store(acc, m, first, width, engine):
-            y = held.tile([P, width], F32, name=f"y{m}_{first}")
+            last = first + width
             r, j = divmod(m, BJ)
             bias_m = bias[:, j, r : r + 1]
             if engine == 0:
-                nc.scalar.activation(y[:], acc[:], IDENTITY, bias=bias_m)
+                nc.scalar.activation(y[m][:, first:last], acc[:], IDENTITY, bias=bias_m)
             else:
-                nc.vector.tensor_scalar_add(y[:], acc[:], bias_m)
-            nc.sync.dma_start(out[C + m * P : C + (m + 1) * P, first : first + width], y[:])
+                nc.vector.tensor_scalar_add(y[m][:, first:last], acc[:], bias_m)
+            if m >= 2 * QB:
+                nc.sync.dma_start(out[C + m * P : C + (m + 1) * P, first:last], y[m][:, first:last])
+            elif last == N:
+                nc.sync.dma_start(out[C + m * P : C + (m + 1) * P, :], y[m][:])
 
         x32 = held.tile([P, KB, N], F32, name="x32")
         x16 = [held.tile([P, N], BF16, name=f"x16_{k}") for k in range(KB)]
@@ -103,7 +109,7 @@ def tile_plaindecoder_kernel(tc, emb, pos, wqkv, bqkv, offs, out):
                 add_bias_and_store(q_acc[m][h], m, h * HALF, HALF, 1 - h)
 
         for m in range(QB, MB):
-            widths = [HALF, HALF] if m < MB - 1 else [HALF, HALF - T, T]
+            widths = [HALF, HALF] if m < MB - 1 else [HALF, HALF - LAST, LAST]
             first = 0
             for j, width in enumerate(widths):
                 acc = psum.tile([P, width], F32, name="acc")

@@ -56,10 +56,10 @@ def tile_plaindecoder_kernel(tc, emb, pos, wqkv, bqkv, offs, out):
         bias = held.tile([P, BJ, BR], F32, name="bias")
         nc.vector.tensor_copy(bias[:], bias_t[:])
 
-        pos_rep = [held.tile([P, HALF // T, T], F32, name=f"pos_rep{k}") for k in range(KB)]
+        pos_rep = [held.tile([P, QUARTER // T, T], F32, name=f"pos_rep{k}") for k in range(KB)]
         for k in range(KB):
             nc.scalar.activation(
-                pos_rep[k][:], pos_sb[:, k, :].unsqueeze(1).to_broadcast([P, HALF // T, T]), COPY
+                pos_rep[k][:], pos_sb[:, k, :].unsqueeze(1).to_broadcast([P, QUARTER // T, T]), COPY
             )
 
         y = [held.tile([P, N], F32, name=f"y{m}") for m in range(MB)]
@@ -93,7 +93,10 @@ def tile_plaindecoder_kernel(tc, emb, pos, wqkv, bqkv, offs, out):
                 nc.vector.tensor_tensor(
                     x32[:, k, cols], emb_sb[k][:].indirect(piece), pos_rep[k][:, 0 : width // T, :], ADD
                 )
-                nc.scalar.activation(x16[k][:, cols], x32[:, k, cols], COPY)
+                if k == KB - 1 and first >= N - QUARTER:
+                    nc.vector.tensor_copy(x16[k][:, cols], x32[:, k, cols])
+                else:
+                    nc.scalar.activation(x16[k][:, cols], x32[:, k, cols], COPY)
                 h, inside = divmod(first, HALF)
                 for m in range(QB):
                     nc.tensor.matmul(
@@ -106,7 +109,7 @@ def tile_plaindecoder_kernel(tc, emb, pos, wqkv, bqkv, offs, out):
         nc.sync.dma_start(x_v, x32[:])
         for m in range(QB):
             for h in range(NH):
-                add_bias_and_store(q_acc[m][h], m, h * HALF, HALF, 1 - h)
+                add_bias_and_store(q_acc[m][h], m, h * HALF, HALF, h)
 
         for m in range(QB, MB):
             widths = [HALF, HALF] if m < MB - 1 else [HALF, HALF - LAST, LAST]

@@ -14,6 +14,7 @@ QB = 4
 HALF = 512
 NH = N // HALF
 QUARTER = HALF // 2
+KE = 2
 LAST = 224
 BR = 4
 BJ = MB // BR
@@ -38,10 +39,11 @@ def tile_plaindecoder_kernel(tc, emb, pos, wqkv, bqkv, offs, out):
         pos_sb = held.tile([P, KB, T], F32, name="pos_sb")
         nc.sync.dma_start(pos_sb[:, 0 : KB // 2, :], pos_v[:, 0 : KB // 2, :])
         emb_sb = [held.tile([P, S], F32, name=f"emb{k}") for k in range(KB)]
-        w_q = [held.tile([P, QB * P], BF16, name=f"w_q{k}") for k in range(KB)]
+        q_cols = [(QB + 1) * P if k < KE else QB * P for k in range(KB)]
+        w_q = [held.tile([P, q_cols[k]], BF16, name=f"w_q{k}") for k in range(KB)]
         for k in range(KB):
             nc.sync.dma_start(emb_sb[k][:], emb_v[:, k, :])
-            nc.sync.dma_start(w_q[k][:], w_v[:, k, 0 : QB * P])
+            nc.sync.dma_start(w_q[k][:], w_v[:, k, 0 : q_cols[k]])
             if k == 0:
                 nc.sync.dma_start(pos_sb[:, KB // 2 : KB, :], pos_v[:, KB // 2 : KB, :])
         w_kv = [held.tile([P, KB, QB * P], BF16, name=f"w_kv{g}") for g in range(2)]
@@ -64,14 +66,18 @@ def tile_plaindecoder_kernel(tc, emb, pos, wqkv, bqkv, offs, out):
 
         y = [held.tile([P, N], F32, name=f"y{m}") for m in range(MB)]
 
+        def bias_of(m):
+            r, j = divmod(m, BJ)
+            return bias[:, j, r : r + 1]
+
         def add_bias_and_store(acc, m, first, width, engine):
             last = first + width
-            r, j = divmod(m, BJ)
-            bias_m = bias[:, j, r : r + 1]
-            if engine == 0:
-                nc.scalar.activation(y[m][:, first:last], acc[:], IDENTITY, bias=bias_m)
+            if m == QB and first == 0:
+                nc.vector.tensor_add(y[m][:, first:last], acc[:], parked[:])
+            elif engine == 0:
+                nc.scalar.activation(y[m][:, first:last], acc[:], IDENTITY, bias=bias_of(m))
             else:
-                nc.vector.tensor_scalar_add(y[m][:, first:last], acc[:], bias_m)
+                nc.vector.tensor_scalar_add(y[m][:, first:last], acc[:], bias_of(m))
             if m >= 2 * QB:
                 nc.sync.dma_start(out[C + m * P : C + (m + 1) * P, first:last], y[m][:, first:last])
             elif last == N:
@@ -79,7 +85,10 @@ def tile_plaindecoder_kernel(tc, emb, pos, wqkv, bqkv, offs, out):
 
         x32 = held.tile([P, KB, N], F32, name="x32")
         x16 = [held.tile([P, N], BF16, name=f"x16_{k}") for k in range(KB)]
+        parked = held.tile([P, HALF], F32, name="parked")
+        early = psum.tile([P, HALF], F32, name="early", tag="acc")
         q_acc = [[psum.tile([P, HALF], F32, name="acc") for h in range(NH)] for m in range(QB)]
+        late = q_acc[QB - 1][NH - 1]
         for k in range(KB):
             widths = [QUARTER] * 4
             if k == 0:
@@ -99,6 +108,8 @@ def tile_plaindecoder_kernel(tc, emb, pos, wqkv, bqkv, offs, out):
                     nc.scalar.activation(x16[k][:, cols], x32[:, k, cols], COPY)
                 h, inside = divmod(first, HALF)
                 for m in range(QB):
+                    if q_acc[m][h] is late and k < KE:
+                        continue
                     nc.tensor.matmul(
                         q_acc[m][h][:, inside : inside + width],
                         w_q[k][:, m * P : (m + 1) * P],
@@ -106,6 +117,18 @@ def tile_plaindecoder_kernel(tc, emb, pos, wqkv, bqkv, offs, out):
                         start=(k == 0 and inside == 0),
                         stop=(k == KB - 1 and inside + width == HALF),
                     )
+                if inside + width == HALF and h == 0:
+                    if k < KE:
+                        nc.tensor.matmul(
+                            early[:], w_q[k][:, QB * P :], x16[k][:, 0:HALF], start=(k == 0), stop=(k == KE - 1)
+                        )
+                    if k == KE - 1:
+                        nc.scalar.activation(parked[:], early[:], IDENTITY, bias=bias_of(QB))
+                    if k == KE:
+                        for j in range(KE):
+                            nc.tensor.matmul(
+                                late[:], w_q[j][:, (QB - 1) * P : QB * P], x16[j][:, HALF:N], start=(j == 0), stop=False
+                            )
         nc.sync.dma_start(x_v, x32[:])
         for m in range(QB):
             for h in range(NH):
@@ -116,13 +139,14 @@ def tile_plaindecoder_kernel(tc, emb, pos, wqkv, bqkv, offs, out):
             first = 0
             for j, width in enumerate(widths):
                 acc = psum.tile([P, width], F32, name="acc")
-                for k in range(KB):
+                k0 = KE if m == QB and first == 0 else 0
+                for k in range(k0, KB):
                     nc.tensor.matmul(
                         acc[:],
                         w_kv[m // QB - 1][:, k, (m % QB) * P : (m % QB + 1) * P],
                         x16[k][:, first : first + width],
-                        start=(k == 0),
+                        start=(k == k0),
                         stop=(k == KB - 1),
                     )
-                add_bias_and_store(acc, m, first, width, (len(widths) - j) % 2)
+                add_bias_and_store(acc, m, first, width, 0 if m == QB else (len(widths) - j) % 2)
                 first += width

@@ -72,8 +72,8 @@ def tile_plaindecoder_kernel(tc, emb, pos, wqkv, bqkv, offs, out):
 
         def add_bias_and_store(acc, m, first, width, engine):
             last = first + width
-            if m == QB and first == 0:
-                nc.vector.tensor_add(y[m][:, first:last], acc[:], parked[:])
+            if m == QB:
+                nc.vector.tensor_add(y[m][:, first:last], acc[:], parked[:, first:last])
             elif engine == 0:
                 nc.scalar.activation(y[m][:, first:last], acc[:], IDENTITY, bias=bias_of(m))
             else:
@@ -85,10 +85,9 @@ def tile_plaindecoder_kernel(tc, emb, pos, wqkv, bqkv, offs, out):
 
         x32 = held.tile([P, KB, N], F32, name="x32")
         x16 = [held.tile([P, N], BF16, name=f"x16_{k}") for k in range(KB)]
-        parked = held.tile([P, HALF], F32, name="parked")
-        early = psum.tile([P, HALF], F32, name="early", tag="acc")
+        parked = held.tile([P, N], F32, name="parked")
+        early = [psum.tile([P, HALF], F32, name="early", tag="acc") for h in range(NH)]
         q_acc = [[psum.tile([P, HALF], F32, name="acc") for h in range(NH)] for m in range(QB)]
-        late = q_acc[QB - 1][NH - 1]
         for k in range(KB):
             widths = [QUARTER] * 4
             if k == 0:
@@ -107,9 +106,16 @@ def tile_plaindecoder_kernel(tc, emb, pos, wqkv, bqkv, offs, out):
                 else:
                     nc.scalar.activation(x16[k][:, cols], x32[:, k, cols], COPY)
                 h, inside = divmod(first, HALF)
-                for m in range(QB):
-                    if q_acc[m][h] is late and k < KE:
-                        continue
+                if k == KE and inside == 0:
+                    for j in range(KE):
+                        nc.tensor.matmul(
+                            q_acc[QB - 1][h][:],
+                            w_q[j][:, (QB - 1) * P : QB * P],
+                            x16[j][:, h * HALF : (h + 1) * HALF],
+                            start=(j == 0),
+                            stop=False,
+                        )
+                for m in range(QB if k >= KE else QB - 1):
                     nc.tensor.matmul(
                         q_acc[m][h][:, inside : inside + width],
                         w_q[k][:, m * P : (m + 1) * P],
@@ -117,18 +123,13 @@ def tile_plaindecoder_kernel(tc, emb, pos, wqkv, bqkv, offs, out):
                         start=(k == 0 and inside == 0),
                         stop=(k == KB - 1 and inside + width == HALF),
                     )
-                if inside + width == HALF and h == 0:
-                    if k < KE:
-                        nc.tensor.matmul(
-                            early[:], w_q[k][:, QB * P :], x16[k][:, 0:HALF], start=(k == 0), stop=(k == KE - 1)
-                        )
+                if inside + width == HALF and k < KE:
+                    half = slice(h * HALF, (h + 1) * HALF)
+                    nc.tensor.matmul(
+                        early[h][:], w_q[k][:, QB * P :], x16[k][:, half], start=(k == 0), stop=(k == KE - 1)
+                    )
                     if k == KE - 1:
-                        nc.scalar.activation(parked[:], early[:], IDENTITY, bias=bias_of(QB))
-                    if k == KE:
-                        for j in range(KE):
-                            nc.tensor.matmul(
-                                late[:], w_q[j][:, (QB - 1) * P : QB * P], x16[j][:, HALF:N], start=(j == 0), stop=False
-                            )
+                        nc.scalar.activation(parked[:, half], early[h][:], IDENTITY, bias=bias_of(QB))
         nc.sync.dma_start(x_v, x32[:])
         for m in range(QB):
             for h in range(NH):
@@ -139,7 +140,7 @@ def tile_plaindecoder_kernel(tc, emb, pos, wqkv, bqkv, offs, out):
             first = 0
             for j, width in enumerate(widths):
                 acc = psum.tile([P, width], F32, name="acc")
-                k0 = KE if m == QB and first == 0 else 0
+                k0 = KE if m == QB else 0
                 for k in range(k0, KB):
                     nc.tensor.matmul(
                         acc[:],
@@ -148,5 +149,5 @@ def tile_plaindecoder_kernel(tc, emb, pos, wqkv, bqkv, offs, out):
                         start=(k == k0),
                         stop=(k == KB - 1),
                     )
-                add_bias_and_store(acc, m, first, width, 0 if m == QB else (len(widths) - j) % 2)
+                add_bias_and_store(acc, m, first, width, (len(widths) - j) % 2)
                 first += width

import concourse.mybir as mybir
from concourse.masks import make_identity

F32, BF16, U16 = mybir.dt.float32, mybir.dt.bfloat16, mybir.dt.uint16
ADD = mybir.AluOpType.add
COPY = mybir.ActivationFunctionType.Copy
IDENTITY = mybir.ActivationFunctionType.Identity

P = 128
C, S, N, T, E = 512, 2048, 1024, 128, 1536
KB = C // P
MB = E // P
QB = 4
HALF = 512
NH = N // HALF
QUARTER = HALF // 2
KE = 2
LAST = 224
BR = 4
BJ = MB // BR

FLOPS = 2 * C * E * N


def tile_plaindecoder_kernel(tc, emb, pos, wqkv, bqkv, offs, out):
    nc = tc.nc
    emb_v = emb.rearrange("(p k) s -> p k s", k=KB)
    pos_v = pos.rearrange("(p k) t -> p k t", k=KB)
    w_v = wqkv.rearrange("(p k) e -> p k e", k=KB)
    x_v = out[0:C, :].rearrange("(p k) n -> p k n", k=KB)
    with (
        tc.tile_pool(name="held", bufs=1) as held,
        tc.psum_pool(name="psum", bufs=8) as psum,
    ):
        offsets = held.tile([P, N // 16], U16, name="offsets")
        nc.sync.dma_start(offsets[:], offs)
        bias_rows = held.tile([BR, BJ * P], F32, name="bias_rows")
        nc.scalar.dma_start(bias_rows[:], bqkv.rearrange("(r f) o -> r (f o)", r=BR))
        pos_sb = held.tile([P, KB, T], F32, name="pos_sb")
        nc.sync.dma_start(pos_sb[:, 0 : KB // 2, :], pos_v[:, 0 : KB // 2, :])
        emb_sb = [held.tile([P, S], F32, name=f"emb{k}") for k in range(KB)]
        q_cols = [(QB + 1) * P if k < KE else QB * P for k in range(KB)]
        w_q = [held.tile([P, q_cols[k]], BF16, name=f"w_q{k}") for k in range(KB)]
        for k in range(KB):
            nc.sync.dma_start(emb_sb[k][:], emb_v[:, k, :])
            nc.sync.dma_start(w_q[k][:], w_v[:, k, 0 : q_cols[k]])
            if k == 0:
                nc.sync.dma_start(pos_sb[:, KB // 2 : KB, :], pos_v[:, KB // 2 : KB, :])
        w_kv = [held.tile([P, KB, QB * P], BF16, name=f"w_kv{g}") for g in range(2)]
        for g in range(2):
            nc.sync.dma_start(w_kv[g][:], w_v[:, :, (g + 1) * QB * P : (g + 2) * QB * P])

        identity = held.tile([BR, BR], F32, name="identity")
        make_identity(nc, identity[:])
        bias_t = psum.tile([P, BJ, BR], F32, name="bias_t", tag="acc")
        for j in range(BJ):
            nc.tensor.matmul(bias_t[:, j, :], bias_rows[:, j * P : (j + 1) * P], identity[:])
        bias = held.tile([P, BJ, BR], F32, name="bias")
        nc.vector.tensor_copy(bias[:], bias_t[:])

        pos_rep = [held.tile([P, QUARTER // T, T], F32, name=f"pos_rep{k}") for k in range(KB)]
        for k in range(KB):
            nc.scalar.activation(
                pos_rep[k][:], pos_sb[:, k, :].unsqueeze(1).to_broadcast([P, QUARTER // T, T]), COPY
            )

        y = [held.tile([P, N], F32, name=f"y{m}") for m in range(MB)]

        def bias_of(m):
            r, j = divmod(m, BJ)
            return bias[:, j, r : r + 1]

        def add_bias_and_store(acc, m, first, width, engine):
            last = first + width
            if m == QB:
                nc.vector.tensor_add(y[m][:, first:last], acc[:], parked[:, first:last])
            elif engine == 0:
                nc.scalar.activation(y[m][:, first:last], acc[:], IDENTITY, bias=bias_of(m))
            else:
                nc.vector.tensor_scalar_add(y[m][:, first:last], acc[:], bias_of(m))
            if m >= 2 * QB:
                nc.sync.dma_start(out[C + m * P : C + (m + 1) * P, first:last], y[m][:, first:last])
            elif last == N:
                nc.sync.dma_start(out[C + m * P : C + (m + 1) * P, :], y[m][:])

        x32 = held.tile([P, KB, N], F32, name="x32")
        x16 = [held.tile([P, N], BF16, name=f"x16_{k}") for k in range(KB)]
        parked = held.tile([P, N], F32, name="parked")
        early = [psum.tile([P, HALF], F32, name="early", tag="acc") for h in range(NH)]
        q_acc = [[psum.tile([P, HALF], F32, name="acc") for h in range(NH)] for m in range(QB)]
        for k in range(KB):
            widths = [QUARTER] * 4
            if k == 0:
                widths = [T, T] + [QUARTER] * 3
            if k == KB - 1:
                widths = [QUARTER] * 3 + [T, T]
            for i, width in enumerate(widths):
                first = sum(widths[:i])
                cols = slice(first, first + width)
                piece = offsets[:, first // 16 : (first + width) // 16]
                nc.vector.tensor_tensor(
                    x32[:, k, cols], emb_sb[k][:].indirect(piece), pos_rep[k][:, 0 : width // T, :], ADD
                )
                if k == KB - 1 and first >= N - QUARTER:
                    nc.vector.tensor_copy(x16[k][:, cols], x32[:, k, cols])
                else:
                    nc.scalar.activation(x16[k][:, cols], x32[:, k, cols], COPY)
                h, inside = divmod(first, HALF)
                if k == KE and inside == 0:
                    for j in range(KE):
                        nc.tensor.matmul(
                            q_acc[QB - 1][h][:],
                            w_q[j][:, (QB - 1) * P : QB * P],
                            x16[j][:, h * HALF : (h + 1) * HALF],
                            start=(j == 0),
                            stop=False,
                        )
                for m in range(QB if k >= KE else QB - 1):
                    nc.tensor.matmul(
                        q_acc[m][h][:, inside : inside + width],
                        w_q[k][:, m * P : (m + 1) * P],
                        x16[k][:, cols],
                        start=(k == 0 and inside == 0),
                        stop=(k == KB - 1 and inside + width == HALF),
                    )
                if inside + width == HALF and k < KE:
                    half = slice(h * HALF, (h + 1) * HALF)
                    nc.tensor.matmul(
                        early[h][:], w_q[k][:, QB * P :], x16[k][:, half], start=(k == 0), stop=(k == KE - 1)
                    )
                    if k == KE - 1:
                        nc.scalar.activation(parked[:, half], early[h][:], IDENTITY, bias=bias_of(QB))
        nc.sync.dma_start(x_v, x32[:])
        for m in range(QB):
            for h in range(NH):
                add_bias_and_store(q_acc[m][h], m, h * HALF, HALF, h)

        for m in range(QB, MB):
            widths = [HALF, HALF] if m < MB - 1 else [HALF, HALF - LAST, LAST]
            first = 0
            for j, width in enumerate(widths):
                acc = psum.tile([P, width], F32, name="acc")
                k0 = KE if m == QB else 0
                for k in range(k0, KB):
                    nc.tensor.matmul(
                        acc[:],
                        w_kv[m // QB - 1][:, k, (m % QB) * P : (m % QB + 1) * P],
                        x16[k][:, first : first + width],
                        start=(k == k0),
                        stop=(k == KB - 1),
                    )
                add_bias_and_store(acc, m, first, width, (len(widths) - j) % 2)
                first += width
